import numpy as np
import ml_dtypes


def mxq(x, axis, fmt="e4m3"):
    dtype, down = {"e4m3": (ml_dtypes.float8_e4m3fn, 7), "e5m2": (ml_dtypes.float8_e5m2, 14)}[fmt]
    v = np.moveaxis(np.asarray(x, np.float32).astype(ml_dtypes.bfloat16).astype(np.float64), axis, -1)
    blocks = v.reshape(v.shape[:-1] + (-1, 32))
    amax = np.abs(blocks).max(-1, keepdims=True)
    byte = np.maximum(np.where(amax > 0, np.frexp(amax)[1] - 1 + 127, 0) - down, 1)
    scale = np.exp2(byte - 127.0)
    codes = (blocks / scale).astype(np.float32).astype(dtype).astype(np.float64)
    return np.moveaxis((codes * scale).reshape(v.shape), -1, axis)


WIDE = False


def mx_kscale(k):
    if not WIDE:
        return np.ones(k)
    levels = np.array([10, -10, 5, -5, 0])
    a = np.random.permutation(np.resize(levels, k // 512 * 4)).reshape(k // 512, 4)
    idx = np.arange(k)
    return np.exp2(a[idx // 512, idx % 128 // 32])


BF16 = ml_dtypes.bfloat16


def bf(x):
    return np.asarray(x, np.float32).astype(BF16)


def f64(x):
    return np.asarray(x).astype(np.float64)


B, T, N, DH, D = 4, 1024, 16, 32, 512
KC = N * DH


def setup_inputs():
    r = np.random.standard_normal
    s = mx_kscale(D)
    t = mx_kscale(KC).reshape(N, DH)
    return {"normalized_resid_pre": bf(r((B, T, D)) * s),
            "W_C": bf(r((N, D, DH)) / np.sqrt(D) / s[None, :, None] * t[:, None, :]),
            "b_C": bf(0.1 * r((N, DH)) * t),
            "W_K": bf(1.3 / np.sqrt(KC) * r((N, DH, DH, DH)) / t[:, None, None, :])}


def reference(normalized_resid_pre, W_C, b_C, W_K):
    x = f64(normalized_resid_pre)
    wc = f64(W_C).transpose(1, 0, 2).reshape(D, KC)
    c = (mxq(x, 2, "e4m3") @ mxq(wc, 0, "e4m3")) + f64(b_C).reshape(KC)
    wk = f64(W_K).transpose(0, 3, 1, 2).reshape(KC, DH * DH)
    step1 = mxq(c, 2, "e4m3") @ mxq(wk, 0, "e4m3")
    return step1.reshape(B, T, DH, DH)

@@ -1,0 +1,226 @@
+from contextlib import ExitStack
+
+import concourse.mybir as mybir
+from concourse.masks import make_identity
+
+BF16 = mybir.dt.bfloat16
+F32 = mybir.dt.float32
+U32 = mybir.dt.uint32
+U8 = mybir.dt.uint8
+FP8X4 = mybir.dt.float8_e4m3fn_x4
+
+P = 128
+PACK = 4
+ROWS = 4 * 1024
+D = 512
+HEADS = 16
+DH = 32
+KK = HEADS * DH
+IJ = DH * DH
+BANK = 512
+
+TILES_IN_CHUNK = 4
+CHUNK = TILES_IN_CHUNK * P
+CHUNKS = ROWS // CHUNK
+ROW_TILES = ROWS // P
+TILES_IN_STORE = 2
+IJ_IN_RUN = IJ // P
+
+FLOPS = 2 * ROWS * D * KK + 2 * ROWS * KK * IJ
+
+
+def tile_trittentioncube_pa_t_kernel(tc, normalized_resid_pre, W_C, b_C, W_K, out):
+    nc = tc.nc
+    x_rows = normalized_resid_pre.flatten_outer_dims()
+    out_rows = out.rearrange("b r i j -> (b r) (i j)")
+
+    with ExitStack() as stack:
+        keep = stack.enter_context(tc.tile_pool(name="keep", bufs=1))
+        x_pool = stack.enter_context(tc.tile_pool(name="x_pool", bufs=CHUNKS))
+        xq_pool = stack.enter_context(tc.tile_pool(name="xq_pool", bufs=3))
+        cq_pool = stack.enter_context(tc.tile_pool(name="cq_pool", bufs=4))
+        out_pool = stack.enter_context(tc.tile_pool(name="out_pool", bufs=4))
+        xt_banks = stack.enter_context(tc.psum_pool(name="xt_banks", bufs=2))
+        c_banks = stack.enter_context(tc.psum_pool(name="c_banks", bufs=2))
+        out_banks = stack.enter_context(tc.psum_pool(name="out_banks", bufs=4))
+
+        wc_raw = keep.tile([P, HEADS, PACK, DH], BF16)
+        nc.sync.dma_start(
+            out=wc_raw[:].rearrange("p n (u e) k -> p n u e k", e=2),
+            in_=W_C.rearrange("n (u p e) k -> p n u e k", u=2, e=2),
+        )
+        x_chunks = []
+
+        def load_x(i):
+            x_sb = x_pool.tile([P, TILES_IN_CHUNK, D], BF16)
+            nc.sync.dma_start(
+                out=x_sb[:],
+                in_=x_rows[i * CHUNK : (i + 1) * CHUNK, :].rearrange("(p a) d -> p a d", a=TILES_IN_CHUNK),
+            )
+            x_chunks.append(x_sb)
+
+        load_x(0)
+        wk_raw = keep.tile([P, HEADS, IJ_IN_RUN, DH], BF16)
+        nc.sync.dma_start(
+            out=wk_raw[:],
+            in_=W_K.rearrange("n i j k -> n (i j) k").rearrange("n (s c) k -> s n c k", c=IJ_IN_RUN),
+        )
+        for i in range(1, CHUNKS):
+            load_x(i)
+        bias_raw = keep.tile([P, PACK], BF16)
+        nc.scalar.dma_start(out=bias_raw[:], in_=b_C.rearrange("n (q t) -> (n q) t", t=PACK))
+        bias = keep.tile([P, PACK], F32)
+        nc.vector.tensor_copy(out=bias[:], in_=bias_raw[:])
+
+        identity = keep.tile([P, P], F32)
+        make_identity(nc, identity[:])
+
+        wc_grouped = keep.tile([P, PACK, P, PACK], BF16, align_bytes=64)
+        for t in range(PACK):
+            nc.vector.tensor_copy(
+                out=wc_grouped[:, t].rearrange("p (n q) j -> p n q j", n=HEADS),
+                in_=wc_raw[:].rearrange("p n j (q t) -> p t n q j", t=PACK)[:, t],
+            )
+        wc_codes = keep.tile([P, KK], U32, align_bytes=64)
+        wc_scales = keep.tile([P, KK], U8, align_bytes=64)
+        nc.vector.quantize_mx(
+            out=wc_codes[:].bitcast(FP8X4),
+            scales=wc_scales[:],
+            in_=wc_grouped[:].rearrange("p t m j -> p (t m j)"),
+        )
+
+        x_grouped = {}
+        x_codes = {}
+        x_scales = {}
+        c_grouped = {}
+        c_codes = {}
+        c_scales = {}
+        out_tiles = {}
+
+        def transpose_x(i, copy):
+            grouped = xq_pool.tile([P, CHUNK * PACK], BF16, align_bytes=64)
+            words = grouped[:].bitcast(F32).rearrange("p (b a r u) -> p b a r u", b=2, a=2, u=2)
+            for b in range(2):
+                xt = xt_banks.tile([P, 2, 2, P], F32)
+                for a in range(2):
+                    for u in range(2):
+                        nc.tensor.transpose(
+                            xt[:, a, u, :],
+                            x_chunks[i][:, 2 * b + a, :].bitcast(F32)[:, u * P : (u + 1) * P],
+                            identity[:],
+                        )
+                copy(out=words[:, b], in_=xt[:].rearrange("p a u r -> p a r u"))
+            x_grouped[i] = grouped
+
+        def quantise_x(i):
+            codes = xq_pool.tile([P, CHUNK], U32, align_bytes=64)
+            scales = xq_pool.tile([P, CHUNK], U8, align_bytes=64)
+            nc.vector.quantize_mx(out=codes[:].bitcast(FP8X4), scales=scales[:], in_=x_grouped[i][:])
+            x_codes[i] = codes
+            x_scales[i] = scales
+
+        def first_product(g):
+            i, a = divmod(g, TILES_IN_CHUNK)
+            rows = slice(a * P, (a + 1) * P)
+            c_ps = c_banks.tile([P, PACK, P], F32)
+            for t in range(PACK):
+                cols = slice(t * P, (t + 1) * P)
+                nc.tensor.matmul_mx(
+                    out=c_ps[:, t, :],
+                    lhsT=wc_codes[:, cols].bitcast(FP8X4),
+                    lhsT_scale=wc_scales[:, cols],
+                    rhs=x_codes[i][:, rows].bitcast(FP8X4),
+                    rhs_scale=x_scales[i][:, rows],
+                    start=True,
+                    stop=True,
+                )
+            grouped = cq_pool.tile([P, P, PACK], BF16, align_bytes=64)
+            nc.vector.tensor_tensor(
+                out=grouped[:],
+                in0=c_ps[:].rearrange("p t r -> p r t"),
+                in1=bias[:].unsqueeze(1).to_broadcast([P, P, PACK]),
+                op=mybir.AluOpType.add,
+            )
+            c_grouped[g] = grouped
+
+        def quantise_c(g):
+            codes = cq_pool.tile([P, P], U32, align_bytes=64)
+            scales = cq_pool.tile([P, P], U8, align_bytes=64)
+            nc.vector.quantize_mx(
+                out=codes[:].bitcast(FP8X4),
+                scales=scales[:],
+                in_=c_grouped[g][:].rearrange("p r t -> p (r t)"),
+            )
+            c_codes[g] = codes
+            c_scales[g] = scales
+
+        def second_product(g):
+            i, a = divmod(g, TILES_IN_CHUNK)
+            first, place = divmod(g, TILES_IN_STORE)
+            if place == 0:
+                out_sb = out_pool.tile([P, TILES_IN_STORE, IJ], F32)
+                out_tiles[first] = out_sb
+            for h in range(IJ // BANK):
+                cols = slice(h * BANK, (h + 1) * BANK)
+                out_ps = out_banks.tile([P, BANK], F32, tag="out_bank")
+                nc.tensor.matmul_mx(
+                    out=out_ps[:],
+                    lhsT=c_codes[g][:].bitcast(FP8X4),
+                    lhsT_scale=c_scales[g][:],
+                    rhs=wk_codes[:, cols].bitcast(FP8X4),
+                    rhs_scale=wk_scales[:, cols],
+                    start=True,
+                    stop=True,
+                )
+                nc.scalar.copy(out=out_tiles[first][:, place, cols], in_=out_ps[:])
+            if place == TILES_IN_STORE - 1:
+                chunk_rows = out_rows[i * CHUNK : (i + 1) * CHUNK, :].rearrange("(p a) c -> p a c", a=TILES_IN_CHUNK)
+                nc.sync.dma_start(out=chunk_rows[:, a + 1 - TILES_IN_STORE : a + 1, :], in_=out_tiles[first][:])
+
+        transpose_x(0, nc.scalar.copy)
+        quantise_x(0)
+        transpose_x(1, nc.scalar.copy)
+        first_product(0)
+        first_product(1)
+        quantise_x(1)
+        quantise_c(0)
+
+        wk_sorted = keep.tile([P, IJ_IN_RUN, KK], BF16)
+        for half in range(2):
+            some = slice(half * IJ_IN_RUN // 2, (half + 1) * IJ_IN_RUN // 2)
+            nc.vector.tensor_copy(
+                out=wk_sorted[:, some, :].rearrange("p c (n k) -> p c n k", k=DH),
+                in_=wk_raw[:, :, some, :].rearrange("p n c k -> p c n k"),
+            )
+        wk_grouped = keep.tile([P, IJ * PACK], BF16, align_bytes=64)
+        wk_words = wk_grouped[:].bitcast(F32).rearrange("p (s c u) -> p s c u", c=IJ_IN_RUN, u=2)
+        for b in range(IJ_IN_RUN // 2):
+            wkt = out_banks.tile([P, 2, 2, P], F32, tag="out_bank")
+            for c in range(2):
+                for u in range(2):
+                    nc.tensor.transpose(
+                        wkt[:, c, u, :],
+                        wk_sorted[:, 2 * b + c, :].bitcast(F32).rearrange("p (m u) -> p u m", u=2)[:, u, :],
+                        identity[:],
+                    )
+            nc.scalar.copy(out=wk_words[:, :, 2 * b : 2 * b + 2, :], in_=wkt[:].rearrange("p c u s -> p s c u"))
+        wk_codes = keep.tile([P, IJ], U32, align_bytes=64)
+        wk_scales = keep.tile([P, IJ], U8, align_bytes=64)
+        for h in range(IJ // BANK):
+            nc.vector.quantize_mx(
+                out=wk_codes[:, h * BANK : (h + 1) * BANK].bitcast(FP8X4),
+                scales=wk_scales[:, h * BANK : (h + 1) * BANK],
+                in_=wk_grouped[:, h * BANK * PACK : (h + 1) * BANK * PACK],
+            )
+
+        for g in range(ROW_TILES):
+            i, a = divmod(g, TILES_IN_CHUNK)
+            if a == 0 and i + 2 < CHUNKS:
+                transpose_x(i + 2, nc.vector.tensor_copy)
+            if g + 2 < ROW_TILES:
+                first_product(g + 2)
+            if g + 1 < ROW_TILES:
+                quantise_c(g + 1)
+            if a == 2 and i + 2 < CHUNKS:
+                quantise_x(i + 2)
+            second_product(g)

@@ -44,11 +44,8 @@ def tile_trittentioncube_pa_t_kernel(tc, normalized_resid_pre, W_C, b_C, W_K, ou
         c_banks = stack.enter_context(tc.psum_pool(name="c_banks", bufs=2))
         out_banks = stack.enter_context(tc.psum_pool(name="out_banks", bufs=4))
 
-        wc_raw = keep.tile([P, HEADS, PACK, DH], BF16)
-        nc.sync.dma_start(
-            out=wc_raw[:].rearrange("p n (u e) k -> p n u e k", e=2),
-            in_=W_C.rearrange("n (u p e) k -> p n u e k", u=2, e=2),
-        )
+        bias_raw = keep.tile([P, PACK], BF16)
+        nc.scalar.dma_start(out=bias_raw[:], in_=b_C.rearrange("n (q t) -> (n q) t", t=PACK))
         x_chunks = []
 
         def load_x(i):
@@ -60,34 +57,24 @@ def tile_trittentioncube_pa_t_kernel(tc, normalized_resid_pre, W_C, b_C, W_K, ou
             x_chunks.append(x_sb)
 
         load_x(0)
-        wk_raw = keep.tile([P, HEADS, IJ_IN_RUN, DH], BF16)
+        wk_raw = keep.tile([P, HEADS * IJ_IN_RUN * DH], BF16)
         nc.sync.dma_start(
-            out=wk_raw[:],
+            out=wk_raw[:].rearrange("p (n c k) -> p n c k", n=HEADS, c=IJ_IN_RUN),
             in_=W_K.rearrange("n i j k -> n (i j) k").rearrange("n (s c) k -> s n c k", c=IJ_IN_RUN),
+        )
+        wc_raw = keep.tile([P, HEADS, PACK, DH], BF16)
+        nc.sync.dma_start(
+            out=wc_raw[:].rearrange("p n (u e) k -> p n u e k", e=2),
+            in_=W_C.rearrange("n (u p e) k -> p n u e k", u=2, e=2),
         )
         for i in range(1, CHUNKS):
             load_x(i)
-        bias_raw = keep.tile([P, PACK], BF16)
-        nc.scalar.dma_start(out=bias_raw[:], in_=b_C.rearrange("n (q t) -> (n q) t", t=PACK))
+
         bias = keep.tile([P, PACK], F32)
         nc.vector.tensor_copy(out=bias[:], in_=bias_raw[:])
 
         identity = keep.tile([P, P], F32)
         make_identity(nc, identity[:])
-
-        wc_grouped = keep.tile([P, PACK, P, PACK], BF16, align_bytes=64)
-        for t in range(PACK):
-            nc.vector.tensor_copy(
-                out=wc_grouped[:, t].rearrange("p (n q) j -> p n q j", n=HEADS),
-                in_=wc_raw[:].rearrange("p n j (q t) -> p t n q j", t=PACK)[:, t],
-            )
-        wc_codes = keep.tile([P, KK], U32, align_bytes=64)
-        wc_scales = keep.tile([P, KK], U8, align_bytes=64)
-        nc.vector.quantize_mx(
-            out=wc_codes[:].bitcast(FP8X4),
-            scales=wc_scales[:],
-            in_=wc_grouped[:].rearrange("p t m j -> p (t m j)"),
-        )
 
         x_grouped = {}
         x_codes = {}
@@ -97,7 +84,7 @@ def tile_trittentioncube_pa_t_kernel(tc, normalized_resid_pre, W_C, b_C, W_K, ou
         c_scales = {}
         out_tiles = {}
 
-        def transpose_x(i, copy):
+        def transpose_x(i):
             grouped = xq_pool.tile([P, CHUNK * PACK], BF16, align_bytes=64)
             words = grouped[:].bitcast(F32).rearrange("p (b a r u) -> p b a r u", b=2, a=2, u=2)
             for b in range(2):
@@ -109,7 +96,7 @@ def tile_trittentioncube_pa_t_kernel(tc, normalized_resid_pre, W_C, b_C, W_K, ou
                             x_chunks[i][:, 2 * b + a, :].bitcast(F32)[:, u * P : (u + 1) * P],
                             identity[:],
                         )
-                copy(out=words[:, b], in_=xt[:].rearrange("p a u r -> p a r u"))
+                nc.scalar.copy(out=words[:, b], in_=xt[:].rearrange("p a u r -> p a r u"))
             x_grouped[i] = grouped
 
         def quantise_x(i):
@@ -172,55 +159,71 @@ def tile_trittentioncube_pa_t_kernel(tc, normalized_resid_pre, W_C, b_C, W_K, ou
                     start=True,
                     stop=True,
                 )
-                nc.scalar.copy(out=out_tiles[first][:, place, cols], in_=out_ps[:])
+                if place == TILES_IN_STORE - 1 and h == IJ // BANK - 1:
+                    nc.vector.tensor_copy(out=out_tiles[first][:, place, cols], in_=out_ps[:])
+                else:
+                    nc.scalar.copy(out=out_tiles[first][:, place, cols], in_=out_ps[:])
             if place == TILES_IN_STORE - 1:
                 chunk_rows = out_rows[i * CHUNK : (i + 1) * CHUNK, :].rearrange("(p a) c -> p a c", a=TILES_IN_CHUNK)
                 nc.sync.dma_start(out=chunk_rows[:, a + 1 - TILES_IN_STORE : a + 1, :], in_=out_tiles[first][:])
 
-        transpose_x(0, nc.scalar.copy)
+        transpose_x(0)
         quantise_x(0)
-        transpose_x(1, nc.scalar.copy)
-        first_product(0)
-        first_product(1)
-        quantise_x(1)
-        quantise_c(0)
 
-        wk_sorted = keep.tile([P, IJ_IN_RUN, KK], BF16)
-        for half in range(2):
-            some = slice(half * IJ_IN_RUN // 2, (half + 1) * IJ_IN_RUN // 2)
-            nc.vector.tensor_copy(
-                out=wk_sorted[:, some, :].rearrange("p c (n k) -> p c n k", k=DH),
-                in_=wk_raw[:, :, some, :].rearrange("p n c k -> p c n k"),
-            )
+        wk_sorted = keep.tile([P, IJ_IN_RUN * KK], BF16)
+        raw_words = wk_raw[:].bitcast(F32).rearrange("p (n c w) -> p c n w", n=HEADS, c=IJ_IN_RUN)
+        sorted_words = wk_sorted[:].bitcast(F32).rearrange("p (c n w) -> p c n w", c=IJ_IN_RUN, n=HEADS)
+        for b in range(IJ_IN_RUN // 2):
+            nc.scalar.copy(out=sorted_words[:, 2 * b : 2 * b + 2], in_=raw_words[:, 2 * b : 2 * b + 2])
+        every_second = wk_sorted[:].bitcast(F32).rearrange("p (c m u) -> p c u m", c=IJ_IN_RUN, u=2)
         wk_grouped = keep.tile([P, IJ * PACK], BF16, align_bytes=64)
         wk_words = wk_grouped[:].bitcast(F32).rearrange("p (s c u) -> p s c u", c=IJ_IN_RUN, u=2)
         for b in range(IJ_IN_RUN // 2):
             wkt = out_banks.tile([P, 2, 2, P], F32, tag="out_bank")
             for c in range(2):
                 for u in range(2):
-                    nc.tensor.transpose(
-                        wkt[:, c, u, :],
-                        wk_sorted[:, 2 * b + c, :].bitcast(F32).rearrange("p (m u) -> p u m", u=2)[:, u, :],
-                        identity[:],
-                    )
+                    nc.tensor.transpose(wkt[:, c, u, :], every_second[:, 2 * b + c, u, :], identity[:])
             nc.scalar.copy(out=wk_words[:, :, 2 * b : 2 * b + 2, :], in_=wkt[:].rearrange("p c u s -> p s c u"))
         wk_codes = keep.tile([P, IJ], U32, align_bytes=64)
         wk_scales = keep.tile([P, IJ], U8, align_bytes=64)
-        for h in range(IJ // BANK):
+
+        def quantise_wk(h):
             nc.vector.quantize_mx(
                 out=wk_codes[:, h * BANK : (h + 1) * BANK].bitcast(FP8X4),
                 scales=wk_scales[:, h * BANK : (h + 1) * BANK],
                 in_=wk_grouped[:, h * BANK * PACK : (h + 1) * BANK * PACK],
             )
 
+        wc_grouped = keep.tile([P, PACK, P, PACK], BF16, align_bytes=64)
+        for t in range(PACK):
+            nc.vector.tensor_copy(
+                out=wc_grouped[:, t].rearrange("p (n q) j -> p n q j", n=HEADS),
+                in_=wc_raw[:].rearrange("p n j (q t) -> p t n q j", t=PACK)[:, t],
+            )
+        wc_codes = keep.tile([P, KK], U32, align_bytes=64)
+        wc_scales = keep.tile([P, KK], U8, align_bytes=64)
+        nc.vector.quantize_mx(
+            out=wc_codes[:].bitcast(FP8X4),
+            scales=wc_scales[:],
+            in_=wc_grouped[:].rearrange("p t m j -> p (t m j)"),
+        )
+
+        transpose_x(1)
+        first_product(0)
+        first_product(1)
+        quantise_wk(0)
+        quantise_c(0)
+        quantise_wk(1)
+        quantise_x(1)
+
         for g in range(ROW_TILES):
             i, a = divmod(g, TILES_IN_CHUNK)
             if a == 0 and i + 2 < CHUNKS:
-                transpose_x(i + 2, nc.vector.tensor_copy)
+                transpose_x(i + 2)
             if g + 2 < ROW_TILES:
                 first_product(g + 2)
             if g + 1 < ROW_TILES:
                 quantise_c(g + 1)
-            if a == 2 and i + 2 < CHUNKS:
+            if a == 1 and i + 2 < CHUNKS:
                 quantise_x(i + 2)
             second_product(g)

@@ -23,7 +23,7 @@ TILES_IN_CHUNK = 4
 CHUNK = TILES_IN_CHUNK * P
 CHUNKS = ROWS // CHUNK
 ROW_TILES = ROWS // P
-TILES_IN_STORE = 2
+TILES_AHEAD = 3
 IJ_IN_RUN = IJ // P
 
 FLOPS = 2 * ROWS * D * KK + 2 * ROWS * KK * IJ
@@ -35,11 +35,12 @@ def tile_trittentioncube_pa_t_kernel(tc, normalized_resid_pre, W_C, b_C, W_K, ou
     out_rows = out.rearrange("b r i j -> (b r) (i j)")
 
     with ExitStack() as stack:
+        stack.enter_context(tc.manual_schedule())
         keep = stack.enter_context(tc.tile_pool(name="keep", bufs=1))
         x_pool = stack.enter_context(tc.tile_pool(name="x_pool", bufs=CHUNKS))
         xq_pool = stack.enter_context(tc.tile_pool(name="xq_pool", bufs=3))
-        cq_pool = stack.enter_context(tc.tile_pool(name="cq_pool", bufs=4))
-        out_pool = stack.enter_context(tc.tile_pool(name="out_pool", bufs=4))
+        cq_pool = stack.enter_context(tc.tile_pool(name="cq_pool", bufs=6))
+        out_pool = stack.enter_context(tc.tile_pool(name="out_pool", bufs=8))
         xt_banks = stack.enter_context(tc.psum_pool(name="xt_banks", bufs=2))
         c_banks = stack.enter_context(tc.psum_pool(name="c_banks", bufs=2))
         out_banks = stack.enter_context(tc.psum_pool(name="out_banks", bufs=4))
@@ -56,16 +57,16 @@ def tile_trittentioncube_pa_t_kernel(tc, normalized_resid_pre, W_C, b_C, W_K, ou
             )
             x_chunks.append(x_sb)
 
-        load_x(0)
-        wk_raw = keep.tile([P, HEADS * IJ_IN_RUN * DH], BF16)
-        nc.sync.dma_start(
-            out=wk_raw[:].rearrange("p (n c k) -> p n c k", n=HEADS, c=IJ_IN_RUN),
-            in_=W_K.rearrange("n i j k -> n (i j) k").rearrange("n (s c) k -> s n c k", c=IJ_IN_RUN),
-        )
         wc_raw = keep.tile([P, HEADS, PACK, DH], BF16)
         nc.sync.dma_start(
             out=wc_raw[:].rearrange("p n (u e) k -> p n u e k", e=2),
             in_=W_C.rearrange("n (u p e) k -> p n u e k", u=2, e=2),
+        )
+        load_x(0)
+        wk_raw = keep.tile([P, HEADS, IJ_IN_RUN, DH], BF16)
+        nc.sync.dma_start(
+            out=wk_raw[:],
+            in_=W_K.rearrange("n i j k -> n (i j) k").rearrange("n (s c) k -> s n c k", c=IJ_IN_RUN),
         )
         for i in range(1, CHUNKS):
             load_x(i)
@@ -82,7 +83,6 @@ def tile_trittentioncube_pa_t_kernel(tc, normalized_resid_pre, W_C, b_C, W_K, ou
         c_grouped = {}
         c_codes = {}
         c_scales = {}
-        out_tiles = {}
 
         def transpose_x(i):
             grouped = xq_pool.tile([P, CHUNK * PACK], BF16, align_bytes=64)
@@ -143,10 +143,7 @@ def tile_trittentioncube_pa_t_kernel(tc, normalized_resid_pre, W_C, b_C, W_K, ou
 
         def second_product(g):
             i, a = divmod(g, TILES_IN_CHUNK)
-            first, place = divmod(g, TILES_IN_STORE)
-            if place == 0:
-                out_sb = out_pool.tile([P, TILES_IN_STORE, IJ], F32)
-                out_tiles[first] = out_sb
+            out_sb = out_pool.tile([P, IJ], F32)
             for h in range(IJ // BANK):
                 cols = slice(h * BANK, (h + 1) * BANK)
                 out_ps = out_banks.tile([P, BANK], F32, tag="out_bank")
@@ -159,40 +156,12 @@ def tile_trittentioncube_pa_t_kernel(tc, normalized_resid_pre, W_C, b_C, W_K, ou
                     start=True,
                     stop=True,
                 )
-                if place == TILES_IN_STORE - 1 and h == IJ // BANK - 1:
-                    nc.vector.tensor_copy(out=out_tiles[first][:, place, cols], in_=out_ps[:])
+                if g % 2 == 1 and h == 1:
+                    nc.vector.tensor_copy(out=out_sb[:, cols], in_=out_ps[:])
                 else:
-                    nc.scalar.copy(out=out_tiles[first][:, place, cols], in_=out_ps[:])
-            if place == TILES_IN_STORE - 1:
-                chunk_rows = out_rows[i * CHUNK : (i + 1) * CHUNK, :].rearrange("(p a) c -> p a c", a=TILES_IN_CHUNK)
-                nc.sync.dma_start(out=chunk_rows[:, a + 1 - TILES_IN_STORE : a + 1, :], in_=out_tiles[first][:])
-
-        transpose_x(0)
-        quantise_x(0)
-
-        wk_sorted = keep.tile([P, IJ_IN_RUN * KK], BF16)
-        raw_words = wk_raw[:].bitcast(F32).rearrange("p (n c w) -> p c n w", n=HEADS, c=IJ_IN_RUN)
-        sorted_words = wk_sorted[:].bitcast(F32).rearrange("p (c n w) -> p c n w", c=IJ_IN_RUN, n=HEADS)
-        for b in range(IJ_IN_RUN // 2):
-            nc.scalar.copy(out=sorted_words[:, 2 * b : 2 * b + 2], in_=raw_words[:, 2 * b : 2 * b + 2])
-        every_second = wk_sorted[:].bitcast(F32).rearrange("p (c m u) -> p c u m", c=IJ_IN_RUN, u=2)
-        wk_grouped = keep.tile([P, IJ * PACK], BF16, align_bytes=64)
-        wk_words = wk_grouped[:].bitcast(F32).rearrange("p (s c u) -> p s c u", c=IJ_IN_RUN, u=2)
-        for b in range(IJ_IN_RUN // 2):
-            wkt = out_banks.tile([P, 2, 2, P], F32, tag="out_bank")
-            for c in range(2):
-                for u in range(2):
-                    nc.tensor.transpose(wkt[:, c, u, :], every_second[:, 2 * b + c, u, :], identity[:])
-            nc.scalar.copy(out=wk_words[:, :, 2 * b : 2 * b + 2, :], in_=wkt[:].rearrange("p c u s -> p s c u"))
-        wk_codes = keep.tile([P, IJ], U32, align_bytes=64)
-        wk_scales = keep.tile([P, IJ], U8, align_bytes=64)
-
-        def quantise_wk(h):
-            nc.vector.quantize_mx(
-                out=wk_codes[:, h * BANK : (h + 1) * BANK].bitcast(FP8X4),
-                scales=wk_scales[:, h * BANK : (h + 1) * BANK],
-                in_=wk_grouped[:, h * BANK * PACK : (h + 1) * BANK * PACK],
-            )
+                    nc.scalar.copy(out=out_sb[:, cols], in_=out_ps[:])
+            chunk_rows = out_rows[i * CHUNK : (i + 1) * CHUNK, :].rearrange("(p a) c -> p a c", a=TILES_IN_CHUNK)
+            nc.sync.dma_start(out=chunk_rows[:, a, :], in_=out_sb[:])
 
         wc_grouped = keep.tile([P, PACK, P, PACK], BF16, align_bytes=64)
         for t in range(PACK):
@@ -208,22 +177,48 @@ def tile_trittentioncube_pa_t_kernel(tc, normalized_resid_pre, W_C, b_C, W_K, ou
             in_=wc_grouped[:].rearrange("p t m j -> p (t m j)"),
         )
 
-        transpose_x(1)
+        transpose_x(0)
+        quantise_x(0)
+
+        wk_sorted = keep.tile([P, IJ_IN_RUN, KK], BF16)
+        for b in range(IJ_IN_RUN // 2):
+            nc.vector.tensor_copy(
+                out=wk_sorted[:, 2 * b : 2 * b + 2, :].rearrange("p c (n k) -> p c n k", k=DH),
+                in_=wk_raw[:, :, 2 * b : 2 * b + 2, :].rearrange("p n c k -> p c n k"),
+            )
         first_product(0)
         first_product(1)
-        quantise_wk(0)
+        wk_grouped = keep.tile([P, IJ * PACK], BF16, align_bytes=64)
+        wk_words = wk_grouped[:].bitcast(F32).rearrange("p (s c u) -> p s c u", c=IJ_IN_RUN, u=2)
+        for b in range(IJ_IN_RUN // 2):
+            wkt = out_banks.tile([P, 2, 2, P], F32, tag="out_bank")
+            for c in range(2):
+                every_second = wk_sorted[:, 2 * b + c, :].bitcast(F32).rearrange("p (m u) -> p u m", u=2)
+                for u in range(2):
+                    nc.tensor.transpose(wkt[:, c, u, :], every_second[:, u, :], identity[:])
+            nc.scalar.copy(out=wk_words[:, :, 2 * b : 2 * b + 2, :], in_=wkt[:].rearrange("p c u s -> p s c u"))
         quantise_c(0)
-        quantise_wk(1)
+        quantise_c(1)
+        transpose_x(1)
+        wk_codes = keep.tile([P, IJ], U32, align_bytes=64)
+        wk_scales = keep.tile([P, IJ], U8, align_bytes=64)
+        for h in range(IJ // BANK):
+            nc.vector.quantize_mx(
+                out=wk_codes[:, h * BANK : (h + 1) * BANK].bitcast(FP8X4),
+                scales=wk_scales[:, h * BANK : (h + 1) * BANK],
+                in_=wk_grouped[:, h * BANK * PACK : (h + 1) * BANK * PACK],
+            )
         quantise_x(1)
+        first_product(2)
 
         for g in range(ROW_TILES):
             i, a = divmod(g, TILES_IN_CHUNK)
             if a == 0 and i + 2 < CHUNKS:
                 transpose_x(i + 2)
-            if g + 2 < ROW_TILES:
-                first_product(g + 2)
-            if g + 1 < ROW_TILES:
-                quantise_c(g + 1)
-            if a == 1 and i + 2 < CHUNKS:
+            if g + TILES_AHEAD < ROW_TILES:
+                first_product(g + TILES_AHEAD)
+            if g + TILES_AHEAD - 1 < ROW_TILES:
+                quantise_c(g + TILES_AHEAD - 1)
+            if a == 2 and i + 2 < CHUNKS:
                 quantise_x(i + 2)
             second_product(g)

@@ -57,16 +57,16 @@ def tile_trittentioncube_pa_t_kernel(tc, normalized_resid_pre, W_C, b_C, W_K, ou
             )
             x_chunks.append(x_sb)
 
-        wc_raw = keep.tile([P, HEADS, PACK, DH], BF16)
-        nc.sync.dma_start(
-            out=wc_raw[:].rearrange("p n (u e) k -> p n u e k", e=2),
-            in_=W_C.rearrange("n (u p e) k -> p n u e k", u=2, e=2),
-        )
         load_x(0)
         wk_raw = keep.tile([P, HEADS, IJ_IN_RUN, DH], BF16)
         nc.sync.dma_start(
             out=wk_raw[:],
             in_=W_K.rearrange("n i j k -> n (i j) k").rearrange("n (s c) k -> s n c k", c=IJ_IN_RUN),
+        )
+        wc_raw = keep.tile([P, HEADS, PACK, DH], BF16)
+        nc.sync.dma_start(
+            out=wc_raw[:].rearrange("p n (u e) k -> p n u e k", e=2),
+            in_=W_C.rearrange("n (u p e) k -> p n u e k", u=2, e=2),
         )
         for i in range(1, CHUNKS):
             load_x(i)
@@ -163,6 +163,25 @@ def tile_trittentioncube_pa_t_kernel(tc, normalized_resid_pre, W_C, b_C, W_K, ou
             chunk_rows = out_rows[i * CHUNK : (i + 1) * CHUNK, :].rearrange("(p a) c -> p a c", a=TILES_IN_CHUNK)
             nc.sync.dma_start(out=chunk_rows[:, a, :], in_=out_sb[:])
 
+        transpose_x(0)
+        quantise_x(0)
+
+        wk_sorted = keep.tile([P, IJ_IN_RUN, KK], BF16)
+        for b in range(IJ_IN_RUN // 2):
+            nc.vector.tensor_copy(
+                out=wk_sorted[:, 2 * b : 2 * b + 2, :].rearrange("p c (n k) -> p c n k", k=DH),
+                in_=wk_raw[:, :, 2 * b : 2 * b + 2, :].rearrange("p n c k -> p c n k"),
+            )
+        wk_grouped = keep.tile([P, IJ * PACK], BF16, align_bytes=64)
+        wk_words = wk_grouped[:].bitcast(F32).rearrange("p (s c u) -> p s c u", c=IJ_IN_RUN, u=2)
+        for b in range(IJ_IN_RUN // 2):
+            wkt = out_banks.tile([P, 2, 2, P], F32, tag="out_bank")
+            for c in range(2):
+                every_second = wk_sorted[:, 2 * b + c, :].bitcast(F32).rearrange("p (m u) -> p u m", u=2)
+                for u in range(2):
+                    nc.tensor.transpose(wkt[:, c, u, :], every_second[:, u, :], identity[:])
+            nc.scalar.copy(out=wk_words[:, :, 2 * b : 2 * b + 2, :], in_=wkt[:].rearrange("p c u s -> p s c u"))
+
         wc_grouped = keep.tile([P, PACK, P, PACK], BF16, align_bytes=64)
         for t in range(PACK):
             nc.vector.tensor_copy(
@@ -177,29 +196,6 @@ def tile_trittentioncube_pa_t_kernel(tc, normalized_resid_pre, W_C, b_C, W_K, ou
             in_=wc_grouped[:].rearrange("p t m j -> p (t m j)"),
         )
 
-        transpose_x(0)
-        quantise_x(0)
-
-        wk_sorted = keep.tile([P, IJ_IN_RUN, KK], BF16)
-        for b in range(IJ_IN_RUN // 2):
-            nc.vector.tensor_copy(
-                out=wk_sorted[:, 2 * b : 2 * b + 2, :].rearrange("p c (n k) -> p c n k", k=DH),
-                in_=wk_raw[:, :, 2 * b : 2 * b + 2, :].rearrange("p n c k -> p c n k"),
-            )
-        first_product(0)
-        first_product(1)
-        wk_grouped = keep.tile([P, IJ * PACK], BF16, align_bytes=64)
-        wk_words = wk_grouped[:].bitcast(F32).rearrange("p (s c u) -> p s c u", c=IJ_IN_RUN, u=2)
-        for b in range(IJ_IN_RUN // 2):
-            wkt = out_banks.tile([P, 2, 2, P], F32, tag="out_bank")
-            for c in range(2):
-                every_second = wk_sorted[:, 2 * b + c, :].bitcast(F32).rearrange("p (m u) -> p u m", u=2)
-                for u in range(2):
-                    nc.tensor.transpose(wkt[:, c, u, :], every_second[:, u, :], identity[:])
-            nc.scalar.copy(out=wk_words[:, :, 2 * b : 2 * b + 2, :], in_=wkt[:].rearrange("p c u s -> p s c u"))
-        quantise_c(0)
-        quantise_c(1)
-        transpose_x(1)
         wk_codes = keep.tile([P, IJ], U32, align_bytes=64)
         wk_scales = keep.tile([P, IJ], U8, align_bytes=64)
         for h in range(IJ // BANK):
@@ -208,6 +204,12 @@ def tile_trittentioncube_pa_t_kernel(tc, normalized_resid_pre, W_C, b_C, W_K, ou
                 scales=wk_scales[:, h * BANK : (h + 1) * BANK],
                 in_=wk_grouped[:, h * BANK * PACK : (h + 1) * BANK * PACK],
             )
+
+        transpose_x(1)
+        first_product(0)
+        first_product(1)
+        quantise_c(0)
+        quantise_c(1)
         quantise_x(1)
         first_product(2)
 

@@ -58,9 +58,9 @@ def tile_trittentioncube_pa_t_kernel(tc, normalized_resid_pre, W_C, b_C, W_K, ou
             x_chunks.append(x_sb)
 
         load_x(0)
-        wk_raw = keep.tile([P, HEADS, IJ_IN_RUN, DH], BF16)
+        wk_raw = keep.tile([P, HEADS * IJ_IN_RUN * DH], BF16)
         nc.sync.dma_start(
-            out=wk_raw[:],
+            out=wk_raw[:].rearrange("p (n c k) -> p n c k", n=HEADS, c=IJ_IN_RUN),
             in_=W_K.rearrange("n i j k -> n (i j) k").rearrange("n (s c) k -> s n c k", c=IJ_IN_RUN),
         )
         wc_raw = keep.tile([P, HEADS, PACK, DH], BF16)
@@ -156,7 +156,7 @@ def tile_trittentioncube_pa_t_kernel(tc, normalized_resid_pre, W_C, b_C, W_K, ou
                     start=True,
                     stop=True,
                 )
-                if g % 2 == 1 and h == 1:
+                if g % 5 in (1, 3) and h == 1:
                     nc.vector.tensor_copy(out=out_sb[:, cols], in_=out_ps[:])
                 else:
                     nc.scalar.copy(out=out_sb[:, cols], in_=out_ps[:])
@@ -166,20 +166,18 @@ def tile_trittentioncube_pa_t_kernel(tc, normalized_resid_pre, W_C, b_C, W_K, ou
         transpose_x(0)
         quantise_x(0)
 
-        wk_sorted = keep.tile([P, IJ_IN_RUN, KK], BF16)
-        for b in range(IJ_IN_RUN // 2):
-            nc.vector.tensor_copy(
-                out=wk_sorted[:, 2 * b : 2 * b + 2, :].rearrange("p c (n k) -> p c n k", k=DH),
-                in_=wk_raw[:, :, 2 * b : 2 * b + 2, :].rearrange("p n c k -> p c n k"),
-            )
+        raw_words = wk_raw[:].bitcast(F32).rearrange("p (n c q u) -> p c u n q", n=HEADS, c=IJ_IN_RUN, u=2)
+        wk_sorted = keep.tile([P, IJ_IN_RUN, 2, P], F32)
+        for c in range(IJ_IN_RUN):
+            copy = nc.vector.tensor_copy if c % 2 == 0 else nc.scalar.copy
+            copy(out=wk_sorted[:, c].rearrange("p u (n q) -> p u n q", n=HEADS), in_=raw_words[:, c])
         wk_grouped = keep.tile([P, IJ * PACK], BF16, align_bytes=64)
         wk_words = wk_grouped[:].bitcast(F32).rearrange("p (s c u) -> p s c u", c=IJ_IN_RUN, u=2)
         for b in range(IJ_IN_RUN // 2):
             wkt = out_banks.tile([P, 2, 2, P], F32, tag="out_bank")
             for c in range(2):
-                every_second = wk_sorted[:, 2 * b + c, :].bitcast(F32).rearrange("p (m u) -> p u m", u=2)
                 for u in range(2):
-                    nc.tensor.transpose(wkt[:, c, u, :], every_second[:, u, :], identity[:])
+                    nc.tensor.transpose(wkt[:, c, u, :], wk_sorted[:, 2 * b + c, u, :], identity[:])
             nc.scalar.copy(out=wk_words[:, :, 2 * b : 2 * b + 2, :], in_=wkt[:].rearrange("p c u s -> p s c u"))
 
         wc_grouped = keep.tile([P, PACK, P, PACK], BF16, align_bytes=64)

from contextlib import ExitStack

import concourse.mybir as mybir
from concourse.masks import make_identity

BF16 = mybir.dt.bfloat16
F32 = mybir.dt.float32
U32 = mybir.dt.uint32
U8 = mybir.dt.uint8
FP8X4 = mybir.dt.float8_e4m3fn_x4

P = 128
PACK = 4
ROWS = 4 * 1024
D = 512
HEADS = 16
DH = 32
KK = HEADS * DH
IJ = DH * DH
BANK = 512

TILES_IN_CHUNK = 4
CHUNK = TILES_IN_CHUNK * P
CHUNKS = ROWS // CHUNK
ROW_TILES = ROWS // P
TILES_AHEAD = 3
IJ_IN_RUN = IJ // P

FLOPS = 2 * ROWS * D * KK + 2 * ROWS * KK * IJ


def tile_trittentioncube_pa_t_kernel(tc, normalized_resid_pre, W_C, b_C, W_K, out):
    nc = tc.nc
    x_rows = normalized_resid_pre.flatten_outer_dims()
    out_rows = out.rearrange("b r i j -> (b r) (i j)")

    with ExitStack() as stack:
        stack.enter_context(tc.manual_schedule())
        keep = stack.enter_context(tc.tile_pool(name="keep", bufs=1))
        x_pool = stack.enter_context(tc.tile_pool(name="x_pool", bufs=CHUNKS))
        xq_pool = stack.enter_context(tc.tile_pool(name="xq_pool", bufs=3))
        cq_pool = stack.enter_context(tc.tile_pool(name="cq_pool", bufs=6))
        out_pool = stack.enter_context(tc.tile_pool(name="out_pool", bufs=8))
        xt_banks = stack.enter_context(tc.psum_pool(name="xt_banks", bufs=2))
        c_banks = stack.enter_context(tc.psum_pool(name="c_banks", bufs=2))
        out_banks = stack.enter_context(tc.psum_pool(name="out_banks", bufs=4))

        bias_raw = keep.tile([P, PACK], BF16)
        nc.scalar.dma_start(out=bias_raw[:], in_=b_C.rearrange("n (q t) -> (n q) t", t=PACK))
        x_chunks = []

        def load_x(i):
            x_sb = x_pool.tile([P, TILES_IN_CHUNK, D], BF16)
            nc.sync.dma_start(
                out=x_sb[:],
                in_=x_rows[i * CHUNK : (i + 1) * CHUNK, :].rearrange("(p a) d -> p a d", a=TILES_IN_CHUNK),
            )
            x_chunks.append(x_sb)

        load_x(0)
        wk_raw = keep.tile([P, HEADS * IJ_IN_RUN * DH], BF16)
        nc.sync.dma_start(
            out=wk_raw[:].rearrange("p (n c k) -> p n c k", n=HEADS, c=IJ_IN_RUN),
            in_=W_K.rearrange("n i j k -> n (i j) k").rearrange("n (s c) k -> s n c k", c=IJ_IN_RUN),
        )
        wc_raw = keep.tile([P, HEADS, PACK, DH], BF16)
        nc.sync.dma_start(
            out=wc_raw[:].rearrange("p n (u e) k -> p n u e k", e=2),
            in_=W_C.rearrange("n (u p e) k -> p n u e k", u=2, e=2),
        )
        for i in range(1, CHUNKS):
            load_x(i)

        bias = keep.tile([P, PACK], F32)
        nc.vector.tensor_copy(out=bias[:], in_=bias_raw[:])

        identity = keep.tile([P, P], F32)
        make_identity(nc, identity[:])

        x_grouped = {}
        x_codes = {}
        x_scales = {}
        c_grouped = {}
        c_codes = {}
        c_scales = {}

        def transpose_x(i):
            grouped = xq_pool.tile([P, CHUNK * PACK], BF16, align_bytes=64)
            words = grouped[:].bitcast(F32).rearrange("p (b a r u) -> p b a r u", b=2, a=2, u=2)
            for b in range(2):
                xt = xt_banks.tile([P, 2, 2, P], F32)
                for a in range(2):
                    for u in range(2):
                        nc.tensor.transpose(
                            xt[:, a, u, :],
                            x_chunks[i][:, 2 * b + a, :].bitcast(F32)[:, u * P : (u + 1) * P],
                            identity[:],
                        )
                nc.scalar.copy(out=words[:, b], in_=xt[:].rearrange("p a u r -> p a r u"))
            x_grouped[i] = grouped

        def quantise_x(i):
            codes = xq_pool.tile([P, CHUNK], U32, align_bytes=64)
            scales = xq_pool.tile([P, CHUNK], U8, align_bytes=64)
            nc.vector.quantize_mx(out=codes[:].bitcast(FP8X4), scales=scales[:], in_=x_grouped[i][:])
            x_codes[i] = codes
            x_scales[i] = scales

        def first_product(g):
            i, a = divmod(g, TILES_IN_CHUNK)
            rows = slice(a * P, (a + 1) * P)
            c_ps = c_banks.tile([P, PACK, P], F32)
            for t in range(PACK):
                cols = slice(t * P, (t + 1) * P)
                nc.tensor.matmul_mx(
                    out=c_ps[:, t, :],
                    lhsT=wc_codes[:, cols].bitcast(FP8X4),
                    lhsT_scale=wc_scales[:, cols],
                    rhs=x_codes[i][:, rows].bitcast(FP8X4),
                    rhs_scale=x_scales[i][:, rows],
                    start=True,
                    stop=True,
                )
            grouped = cq_pool.tile([P, P, PACK], BF16, align_bytes=64)
            nc.vector.tensor_tensor(
                out=grouped[:],
                in0=c_ps[:].rearrange("p t r -> p r t"),
                in1=bias[:].unsqueeze(1).to_broadcast([P, P, PACK]),
                op=mybir.AluOpType.add,
            )
            c_grouped[g] = grouped

        def quantise_c(g):
            codes = cq_pool.tile([P, P], U32, align_bytes=64)
            scales = cq_pool.tile([P, P], U8, align_bytes=64)
            nc.vector.quantize_mx(
                out=codes[:].bitcast(FP8X4),
                scales=scales[:],
                in_=c_grouped[g][:].rearrange("p r t -> p (r t)"),
            )
            c_codes[g] = codes
            c_scales[g] = scales

        def second_product(g):
            i, a = divmod(g, TILES_IN_CHUNK)
            out_sb = out_pool.tile([P, IJ], F32)
            for h in range(IJ // BANK):
                cols = slice(h * BANK, (h + 1) * BANK)
                out_ps = out_banks.tile([P, BANK], F32, tag="out_bank")
                nc.tensor.matmul_mx(
                    out=out_ps[:],
                    lhsT=c_codes[g][:].bitcast(FP8X4),
                    lhsT_scale=c_scales[g][:],
                    rhs=wk_codes[:, cols].bitcast(FP8X4),
                    rhs_scale=wk_scales[:, cols],
                    start=True,
                    stop=True,
                )
                if g % 5 in (1, 3) and h == 1:
                    nc.vector.tensor_copy(out=out_sb[:, cols], in_=out_ps[:])
                else:
                    nc.scalar.copy(out=out_sb[:, cols], in_=out_ps[:])
            chunk_rows = out_rows[i * CHUNK : (i + 1) * CHUNK, :].rearrange("(p a) c -> p a c", a=TILES_IN_CHUNK)
            nc.sync.dma_start(out=chunk_rows[:, a, :], in_=out_sb[:])

        transpose_x(0)
        quantise_x(0)

        raw_words = wk_raw[:].bitcast(F32).rearrange("p (n c q u) -> p c u n q", n=HEADS, c=IJ_IN_RUN, u=2)
        wk_sorted = keep.tile([P, IJ_IN_RUN, 2, P], F32)
        for c in range(IJ_IN_RUN):
            copy = nc.vector.tensor_copy if c % 2 == 0 else nc.scalar.copy
            copy(out=wk_sorted[:, c].rearrange("p u (n q) -> p u n q", n=HEADS), in_=raw_words[:, c])
        wk_grouped = keep.tile([P, IJ * PACK], BF16, align_bytes=64)
        wk_words = wk_grouped[:].bitcast(F32).rearrange("p (s c u) -> p s c u", c=IJ_IN_RUN, u=2)
        for b in range(IJ_IN_RUN // 2):
            wkt = out_banks.tile([P, 2, 2, P], F32, tag="out_bank")
            for c in range(2):
                for u in range(2):
                    nc.tensor.transpose(wkt[:, c, u, :], wk_sorted[:, 2 * b + c, u, :], identity[:])
            nc.scalar.copy(out=wk_words[:, :, 2 * b : 2 * b + 2, :], in_=wkt[:].rearrange("p c u s -> p s c u"))

        wc_grouped = keep.tile([P, PACK, P, PACK], BF16, align_bytes=64)
        for t in range(PACK):
            nc.vector.tensor_copy(
                out=wc_grouped[:, t].rearrange("p (n q) j -> p n q j", n=HEADS),
                in_=wc_raw[:].rearrange("p n j (q t) -> p t n q j", t=PACK)[:, t],
            )
        wc_codes = keep.tile([P, KK], U32, align_bytes=64)
        wc_scales = keep.tile([P, KK], U8, align_bytes=64)
        nc.vector.quantize_mx(
            out=wc_codes[:].bitcast(FP8X4),
            scales=wc_scales[:],
            in_=wc_grouped[:].rearrange("p t m j -> p (t m j)"),
        )

        wk_codes = keep.tile([P, IJ], U32, align_bytes=64)
        wk_scales = keep.tile([P, IJ], U8, align_bytes=64)
        for h in range(IJ // BANK):
            nc.vector.quantize_mx(
                out=wk_codes[:, h * BANK : (h + 1) * BANK].bitcast(FP8X4),
                scales=wk_scales[:, h * BANK : (h + 1) * BANK],
                in_=wk_grouped[:, h * BANK * PACK : (h + 1) * BANK * PACK],
            )

        transpose_x(1)
        first_product(0)
        first_product(1)
        quantise_c(0)
        quantise_c(1)
        quantise_x(1)
        first_product(2)

        for g in range(ROW_TILES):
            i, a = divmod(g, TILES_IN_CHUNK)
            if a == 0 and i + 2 < CHUNKS:
                transpose_x(i + 2)
            if g + TILES_AHEAD < ROW_TILES:
                first_product(g + TILES_AHEAD)
            if g + TILES_AHEAD - 1 < ROW_TILES:
                quantise_c(g + TILES_AHEAD - 1)
            if a == 2 and i + 2 < CHUNKS:
                quantise_x(i + 2)
            second_product(g)
